import numpy as np
import ml_dtypes


def mxq(x, axis, fmt="e4m3"):
    dtype, down = {"e4m3": (ml_dtypes.float8_e4m3fn, 7), "e5m2": (ml_dtypes.float8_e5m2, 14)}[fmt]
    v = np.moveaxis(np.asarray(x, np.float32).astype(ml_dtypes.bfloat16).astype(np.float64), axis, -1)
    blocks = v.reshape(v.shape[:-1] + (-1, 32))
    amax = np.abs(blocks).max(-1, keepdims=True)
    byte = np.maximum(np.where(amax > 0, np.frexp(amax)[1] - 1 + 127, 0) - down, 1)
    scale = np.exp2(byte - 127.0)
    codes = (blocks / scale).astype(np.float32).astype(dtype).astype(np.float64)
    return np.moveaxis((codes * scale).reshape(v.shape), -1, axis)


WIDE = False


def mx_kscale(k):
    if not WIDE:
        return np.ones(k)
    levels = np.array([10, -10, 5, -5, 0])
    a = np.random.permutation(np.resize(levels, k // 512 * 4)).reshape(k // 512, 4)
    idx = np.arange(k)
    return np.exp2(a[idx // 512, idx % 128 // 32])


BF16 = ml_dtypes.bfloat16


def bf(x):
    return np.asarray(x, np.float32).astype(BF16)


def f64(x):
    return np.asarray(x).astype(np.float64)


B, K, D, H1, H2, C = 2048, 2, 1024, 256, 512, 64
N = B * K


def setup_inputs():
    s = mx_kscale(D)
    return {"nf1": bf(np.random.standard_normal((N, D)) * s),
            "nf2": bf(np.random.standard_normal((N * K, D)) * s),
            "w1_0": bf(np.random.standard_normal((D, H1)) / np.sqrt(D) / s[:, None]),
            "w2_0": bf(np.random.standard_normal((D, H1)) / np.sqrt(D) / s[:, None])}


def sage_gcn(cur, neigh, w1, w2):
    b, d = cur.shape
    agg = neigh.reshape(b, -1, d).mean(axis=1)
    return np.maximum((mxq(cur, 1, "e4m3") @ mxq(w2, 0, "e4m3")) + (mxq(agg, 1, "e4m3") @ mxq(w1, 0, "e4m3")), 0.0)


def reference(nf1, nf2, w1_0, w2_0):
    return sage_gcn(f64(nf1), f64(nf2), f64(w1_0), f64(w2_0))

@@ -1,0 +1,165 @@
+from contextlib import ExitStack
+
+import concourse.mybir as mybir
+from concourse.masks import make_identity
+
+F32 = mybir.dt.float32
+BF16 = mybir.dt.bfloat16
+U32 = mybir.dt.uint32
+U8 = mybir.dt.uint8
+FP8X4 = mybir.dt.float8_e4m3fn_x4
+ACT = mybir.ActivationFunctionType
+ALU = mybir.AluOpType
+
+P = 128
+PACK = 4
+K_PASS = P * PACK
+HALVES = 2
+PAIR = 2
+
+NODES = 4096
+NEIGHBOURS = 2
+D = 1024
+H = 256
+PASSES = D // K_PASS
+WORDS = D // PAIR
+
+TILES = 2
+GROUPS = NODES // (P * TILES)
+LOAD_AHEAD = 6
+
+FLOPS = 2 * 2 * NODES * D * H
+
+
+def quantise_weight(nc, const, w, copy, name):
+    raw = const.tile([P, PASSES * PACK * H], BF16, name=name + "_raw")
+    nc.scalar.dma_start(
+        out=raw[:].rearrange("p (s e c) -> p s e c", e=PAIR, c=H),
+        in_=w.rearrange("(s p e) c -> p s e c", p=P, e=PAIR),
+    )
+    grouped = const.tile([P, PASSES * H * PACK], BF16, name=name + "_grouped", align_bytes=64)
+    copy(
+        out=grouped[:].rearrange("p (g c t) -> p g c t", g=PASSES, t=PACK),
+        in_=raw[:].rearrange("p (g t c) -> p g c t", g=PASSES, t=PACK),
+    )
+    codes = const.tile([P, PASSES * H], U32, name=name + "_codes", align_bytes=64)
+    scales = const.tile([P, PASSES * H], U8, name=name + "_scales", align_bytes=64)
+    nc.vector.quantize_mx(out=codes[:].bitcast(FP8X4), scales=scales[:], in_=grouped[:])
+    return codes, scales
+
+
+def tile_graphsage_pa_t_kernel(tc, nf1, nf2, w1_0, w2_0, out):
+    nc = tc.nc
+
+    own_rows = nf1.rearrange("(g p r) d -> g p (r d)", p=P, r=TILES)
+    neighbour_rows = nf2.rearrange("(g p r) d -> g p (r d)", p=P, r=TILES * NEIGHBOURS)
+    out_rows = out.rearrange("(g p r) h -> g p (r h)", p=P, r=TILES)
+
+    with ExitStack() as ctx:
+        ctx.enter_context(tc.manual_schedule())
+        const = ctx.enter_context(tc.tile_pool(name="const", bufs=1))
+        loads = ctx.enter_context(tc.tile_pool(name="loads", bufs=LOAD_AHEAD))
+        work = ctx.enter_context(tc.tile_pool(name="work", bufs=3))
+        psum_t = ctx.enter_context(tc.psum_pool(name="psum_t", bufs=3))
+        psum_acc = ctx.enter_context(tc.psum_pool(name="psum_acc", bufs=2))
+
+        def load(g):
+            neighbours = loads.tile([P, TILES * NEIGHBOURS * D], BF16, name="neighbours")
+            nc.sync.dma_start(out=neighbours[:], in_=neighbour_rows[g])
+            own = loads.tile([P, TILES * D], BF16, name="own")
+            nc.sync.dma_start(out=own[:], in_=own_rows[g])
+            return neighbours, own
+
+        def add_neighbours(neighbours):
+            both = neighbours[:].rearrange("p (r j d) -> p r j d", r=TILES, j=NEIGHBOURS)
+            pair_sum = work.tile([P, TILES * D], BF16, name="pair_sum")
+            nc.vector.tensor_tensor(
+                out=pair_sum[:].rearrange("p (r d) -> p r d", r=TILES),
+                in0=both[:, :, 0, :],
+                in1=both[:, :, 1, :],
+                op=ALU.add,
+            )
+            return pair_sum
+
+        def transpose_words(rows, r, name):
+            words = rows[:].bitcast(F32)
+            bank = psum_t.tile([P, WORDS], F32, name=name)
+            for g in range(PASSES):
+                for u in range(HALVES):
+                    first = r * WORDS + (g * HALVES + u) * P
+                    nc.tensor.transpose(
+                        bank[:, (u * PASSES + g) * P : (u * PASSES + g + 1) * P],
+                        words[:, first : first + P],
+                        identity[:],
+                    )
+            return bank
+
+        def transpose_group(own, pair_sum):
+            mean_banks = [transpose_words(pair_sum, r, "mean_t") for r in range(TILES)]
+            own_banks = [transpose_words(own, r, "own_t") for r in range(TILES)]
+            mean_grouped = work.tile([P, TILES * D], BF16, name="mean_grouped", align_bytes=64)
+            own_grouped = work.tile([P, TILES * D], BF16, name="own_grouped", align_bytes=64)
+            for r in range(TILES):
+                nc.scalar.activation(
+                    out=mean_grouped[:, r * D : (r + 1) * D].rearrange(
+                        "p (n u e) -> p n u e", u=HALVES, e=PAIR
+                    ),
+                    in_=mean_banks[r][:]
+                    .bitcast(BF16)
+                    .rearrange("p (u n e) -> p n u e", u=HALVES, e=PAIR),
+                    func=ACT.Copy,
+                    scale=1.0 / NEIGHBOURS,
+                )
+                nc.vector.tensor_copy(
+                    out=own_grouped[:]
+                    .bitcast(F32)[:, r * WORDS : (r + 1) * WORDS]
+                    .rearrange("p (n u) -> p n u", u=HALVES),
+                    in_=own_banks[r][:].rearrange("p (u n) -> p n u", u=HALVES),
+                )
+            return own_grouped, mean_grouped
+
+        def quantise(grouped, name):
+            codes = work.tile([P, TILES * D // PACK], U32, name=name + "_codes", align_bytes=64)
+            scales = work.tile([P, TILES * D // PACK], U8, name=name + "_scales", align_bytes=64)
+            nc.vector.quantize_mx(out=codes[:].bitcast(FP8X4), scales=scales[:], in_=grouped[:])
+            return codes, scales
+
+        def multiply_and_store(group, own_q, mean_q):
+            products = ((own_q, w2_q), (mean_q, w1_q))
+            acc = psum_acc.tile([P, TILES * H], F32, name="acc")
+            for r in range(TILES):
+                for i, (x_q, w_q) in enumerate(products):
+                    for g in range(PASSES):
+                        nodes = slice((r * PASSES + g) * P, (r * PASSES + g + 1) * P)
+                        cols = slice(g * H, (g + 1) * H)
+                        nc.tensor.matmul_mx(
+                            out=acc[:, r * H : (r + 1) * H],
+                            lhsT=x_q[0][:, nodes].bitcast(FP8X4),
+                            lhsT_scale=x_q[1][:, nodes],
+                            rhs=w_q[0][:, cols].bitcast(FP8X4),
+                            rhs_scale=w_q[1][:, cols],
+                            start=(i == 0 and g == 0),
+                            stop=(i == len(products) - 1 and g == PASSES - 1),
+                        )
+            result = work.tile([P, TILES * H], F32, name="result")
+            nc.scalar.activation(out=result[:], in_=acc[:], func=ACT.Relu)
+            nc.scalar.dma_start(out=out_rows[group], in_=result[:])
+
+        identity = const.tile([P, P], F32, name="identity")
+        make_identity(nc, identity[:])
+        loaded = [load(g) for g in range(LOAD_AHEAD)]
+        w2_q = quantise_weight(nc, const, w2_0, nc.vector.tensor_copy, "w2")
+        w1_q = quantise_weight(nc, const, w1_0, nc.scalar.copy, "w1")
+
+        pair_sums = [add_neighbours(loaded[0][0])]
+        quantised = []
+        for g in range(GROUPS + 1):
+            if g < GROUPS:
+                own_grouped, mean_grouped = transpose_group(loaded[g][1], pair_sums[g])
+                if g + 1 < GROUPS:
+                    pair_sums.append(add_neighbours(loaded[g + 1][0]))
+                quantised.append((quantise(own_grouped, "own"), quantise(mean_grouped, "mean")))
+                if g + LOAD_AHEAD < GROUPS:
+                    loaded.append(load(g + LOAD_AHEAD))
+            if g > 0:
+                multiply_and_store(g - 1, quantised[g - 1][0], quantised[g - 1][1])

@@ -70,7 +70,7 @@ def tile_graphsage_pa_t_kernel(tc, nf1, nf2, w1_0, w2_0, out):
             nc.sync.dma_start(out=own[:], in_=own_rows[g])
             return neighbours, own
 
-        def add_neighbours(neighbours):
+        def mean_of_neighbours(neighbours):
             both = neighbours[:].rearrange("p (r j d) -> p r j d", r=TILES, j=NEIGHBOURS)
             pair_sum = work.tile([P, TILES * D], BF16, name="pair_sum")
             nc.vector.tensor_tensor(
@@ -79,7 +79,9 @@ def tile_graphsage_pa_t_kernel(tc, nf1, nf2, w1_0, w2_0, out):
                 in1=both[:, :, 1, :],
                 op=ALU.add,
             )
-            return pair_sum
+            mean = work.tile([P, TILES * D], BF16, name="mean")
+            nc.vector.tensor_scalar_mul(out=mean[:], in0=pair_sum[:], scalar1=1.0 / NEIGHBOURS)
+            return mean
 
         def transpose_words(rows, r, name):
             words = rows[:].bitcast(F32)
@@ -94,29 +96,17 @@ def tile_graphsage_pa_t_kernel(tc, nf1, nf2, w1_0, w2_0, out):
                     )
             return bank
 
-        def transpose_group(own, pair_sum):
-            mean_banks = [transpose_words(pair_sum, r, "mean_t") for r in range(TILES)]
-            own_banks = [transpose_words(own, r, "own_t") for r in range(TILES)]
-            mean_grouped = work.tile([P, TILES * D], BF16, name="mean_grouped", align_bytes=64)
-            own_grouped = work.tile([P, TILES * D], BF16, name="own_grouped", align_bytes=64)
+        def transpose_group(rows, name):
+            banks = [transpose_words(rows, r, name + "_t") for r in range(TILES)]
+            grouped = work.tile([P, TILES * D], BF16, name=name + "_grouped", align_bytes=64)
             for r in range(TILES):
-                nc.scalar.activation(
-                    out=mean_grouped[:, r * D : (r + 1) * D].rearrange(
-                        "p (n u e) -> p n u e", u=HALVES, e=PAIR
-                    ),
-                    in_=mean_banks[r][:]
-                    .bitcast(BF16)
-                    .rearrange("p (u n e) -> p n u e", u=HALVES, e=PAIR),
-                    func=ACT.Copy,
-                    scale=1.0 / NEIGHBOURS,
-                )
-                nc.vector.tensor_copy(
-                    out=own_grouped[:]
+                nc.scalar.copy(
+                    out=grouped[:]
                     .bitcast(F32)[:, r * WORDS : (r + 1) * WORDS]
                     .rearrange("p (n u) -> p n u", u=HALVES),
-                    in_=own_banks[r][:].rearrange("p (u n) -> p n u", u=HALVES),
+                    in_=banks[r][:].rearrange("p (u n) -> p n u", u=HALVES),
                 )
-            return own_grouped, mean_grouped
+            return grouped
 
         def quantise(grouped, name):
             codes = work.tile([P, TILES * D // PACK], U32, name=name + "_codes", align_bytes=64)
@@ -124,7 +114,7 @@ def tile_graphsage_pa_t_kernel(tc, nf1, nf2, w1_0, w2_0, out):
             nc.vector.quantize_mx(out=codes[:].bitcast(FP8X4), scales=scales[:], in_=grouped[:])
             return codes, scales
 
-        def multiply_and_store(group, own_q, mean_q):
+        def multiply(group, own_q, mean_q):
             products = ((own_q, w2_q), (mean_q, w1_q))
             acc = psum_acc.tile([P, TILES * H], F32, name="acc")
             for r in range(TILES):
@@ -141,25 +131,35 @@ def tile_graphsage_pa_t_kernel(tc, nf1, nf2, w1_0, w2_0, out):
                             start=(i == 0 and g == 0),
                             stop=(i == len(products) - 1 and g == PASSES - 1),
                         )
-            result = work.tile([P, TILES * H], F32, name="result")
-            nc.scalar.activation(out=result[:], in_=acc[:], func=ACT.Relu)
-            nc.scalar.dma_start(out=out_rows[group], in_=result[:])
+            nc.scalar.activation(out=result_of(group), in_=acc[:], func=ACT.Relu)
+
+        def result_of(group):
+            return results[:, group * TILES * H : (group + 1) * TILES * H]
 
         identity = const.tile([P, P], F32, name="identity")
         make_identity(nc, identity[:])
+        results = const.tile([P, GROUPS * TILES * H], F32, name="results")
         loaded = [load(g) for g in range(LOAD_AHEAD)]
+        means = [mean_of_neighbours(loaded[0][0])]
         w2_q = quantise_weight(nc, const, w2_0, nc.vector.tensor_copy, "w2")
         w1_q = quantise_weight(nc, const, w1_0, nc.scalar.copy, "w1")
 
-        pair_sums = [add_neighbours(loaded[0][0])]
         quantised = []
+        stored = 0
         for g in range(GROUPS + 1):
+            if g + 1 < GROUPS:
+                means.append(mean_of_neighbours(loaded[g + 1][0]))
             if g < GROUPS:
-                own_grouped, mean_grouped = transpose_group(loaded[g][1], pair_sums[g])
-                if g + 1 < GROUPS:
-                    pair_sums.append(add_neighbours(loaded[g + 1][0]))
-                quantised.append((quantise(own_grouped, "own"), quantise(mean_grouped, "mean")))
-                if g + LOAD_AHEAD < GROUPS:
-                    loaded.append(load(g + LOAD_AHEAD))
+                mean_grouped = transpose_group(means[g], "mean")
+                own_grouped = transpose_group(loaded[g][1], "own")
+                mean_q = quantise(mean_grouped, "mean")
+                own_q = quantise(own_grouped, "own")
+                quantised.append((own_q, mean_q))
             if g > 0:
-                multiply_and_store(g - 1, quantised[g - 1][0], quantised[g - 1][1])
+                multiply(g - 1, quantised[g - 1][0], quantised[g - 1][1])
+            if g + LOAD_AHEAD < GROUPS:
+                loaded.append(load(g + LOAD_AHEAD))
+            else:
+                for group in range(stored, g):
+                    nc.sync.dma_start(out=out_rows[group], in_=result_of(group))
+                stored = g

@@ -51,9 +51,9 @@ def quantise_weight(nc, const, w, copy, name):
 def tile_graphsage_pa_t_kernel(tc, nf1, nf2, w1_0, w2_0, out):
     nc = tc.nc
 
-    own_rows = nf1.rearrange("(g p r) d -> g p (r d)", p=P, r=TILES)
-    neighbour_rows = nf2.rearrange("(g p r) d -> g p (r d)", p=P, r=TILES * NEIGHBOURS)
-    out_rows = out.rearrange("(g p r) h -> g p (r h)", p=P, r=TILES)
+    own_rows = nf1.rearrange("(p j) d -> p (j d)", p=P)
+    neighbour_rows = nf2.rearrange("(p j) d -> p (j d)", p=P)
+    out_rows = out.rearrange("(p j) h -> p (j h)", p=P)
 
     with ExitStack() as ctx:
         ctx.enter_context(tc.manual_schedule())
@@ -63,11 +63,15 @@ def tile_graphsage_pa_t_kernel(tc, nf1, nf2, w1_0, w2_0, out):
         psum_t = ctx.enter_context(tc.psum_pool(name="psum_t", bufs=3))
         psum_acc = ctx.enter_context(tc.psum_pool(name="psum_acc", bufs=2))
 
+        def columns_of(rows, first_group, end_group):
+            width = rows.shape[1] // GROUPS
+            return rows[:, first_group * width : end_group * width]
+
         def load(g):
             neighbours = loads.tile([P, TILES * NEIGHBOURS * D], BF16, name="neighbours")
-            nc.sync.dma_start(out=neighbours[:], in_=neighbour_rows[g])
+            nc.sync.dma_start(out=neighbours[:], in_=columns_of(neighbour_rows, g, g + 1))
             own = loads.tile([P, TILES * D], BF16, name="own")
-            nc.sync.dma_start(out=own[:], in_=own_rows[g])
+            nc.sync.dma_start(out=own[:], in_=columns_of(own_rows, g, g + 1))
             return neighbours, own
 
         def mean_of_neighbours(neighbours):
@@ -131,10 +135,9 @@ def tile_graphsage_pa_t_kernel(tc, nf1, nf2, w1_0, w2_0, out):
                             start=(i == 0 and g == 0),
                             stop=(i == len(products) - 1 and g == PASSES - 1),
                         )
-            nc.scalar.activation(out=result_of(group), in_=acc[:], func=ACT.Relu)
-
-        def result_of(group):
-            return results[:, group * TILES * H : (group + 1) * TILES * H]
+            nc.scalar.activation(
+                out=columns_of(results, group, group + 1), in_=acc[:], func=ACT.Relu
+            )
 
         identity = const.tile([P, P], F32, name="identity")
         make_identity(nc, identity[:])
@@ -150,16 +153,17 @@ def tile_graphsage_pa_t_kernel(tc, nf1, nf2, w1_0, w2_0, out):
             if g + 1 < GROUPS:
                 means.append(mean_of_neighbours(loaded[g + 1][0]))
             if g < GROUPS:
-                mean_grouped = transpose_group(means[g], "mean")
                 own_grouped = transpose_group(loaded[g][1], "own")
-                mean_q = quantise(mean_grouped, "mean")
+                mean_grouped = transpose_group(means[g], "mean")
                 own_q = quantise(own_grouped, "own")
+                mean_q = quantise(mean_grouped, "mean")
                 quantised.append((own_q, mean_q))
             if g > 0:
                 multiply(g - 1, quantised[g - 1][0], quantised[g - 1][1])
             if g + LOAD_AHEAD < GROUPS:
                 loaded.append(load(g + LOAD_AHEAD))
             else:
-                for group in range(stored, g):
-                    nc.sync.dma_start(out=out_rows[group], in_=result_of(group))
+                nc.sync.dma_start(
+                    out=columns_of(out_rows, stored, g), in_=columns_of(results, stored, g)
+                )
                 stored = g

@@ -26,7 +26,9 @@ WORDS = D // PAIR
 
 TILES = 2
 GROUPS = NODES // (P * TILES)
-LOAD_AHEAD = 6
+LOAD_GROUPS = 2
+LOADS = GROUPS // LOAD_GROUPS
+LOADS_AHEAD = 3
 
 FLOPS = 2 * 2 * NODES * D * H
 
@@ -58,7 +60,7 @@ def tile_graphsage_pa_t_kernel(tc, nf1, nf2, w1_0, w2_0, out):
     with ExitStack() as ctx:
         ctx.enter_context(tc.manual_schedule())
         const = ctx.enter_context(tc.tile_pool(name="const", bufs=1))
-        loads = ctx.enter_context(tc.tile_pool(name="loads", bufs=LOAD_AHEAD))
+        loads = ctx.enter_context(tc.tile_pool(name="loads", bufs=LOADS_AHEAD))
         work = ctx.enter_context(tc.tile_pool(name="work", bufs=3))
         psum_t = ctx.enter_context(tc.psum_pool(name="psum_t", bufs=3))
         psum_acc = ctx.enter_context(tc.psum_pool(name="psum_acc", bufs=2))
@@ -67,15 +69,22 @@ def tile_graphsage_pa_t_kernel(tc, nf1, nf2, w1_0, w2_0, out):
             width = rows.shape[1] // GROUPS
             return rows[:, first_group * width : end_group * width]
 
-        def load(g):
-            neighbours = loads.tile([P, TILES * NEIGHBOURS * D], BF16, name="neighbours")
-            nc.sync.dma_start(out=neighbours[:], in_=columns_of(neighbour_rows, g, g + 1))
-            own = loads.tile([P, TILES * D], BF16, name="own")
-            nc.sync.dma_start(out=own[:], in_=columns_of(own_rows, g, g + 1))
+        def load(n):
+            first, end = n * LOAD_GROUPS, (n + 1) * LOAD_GROUPS
+            neighbours = loads.tile(
+                [P, LOAD_GROUPS * TILES * NEIGHBOURS * D], BF16, name="neighbours"
+            )
+            nc.sync.dma_start(out=neighbours[:], in_=columns_of(neighbour_rows, first, end))
+            own = loads.tile([P, LOAD_GROUPS * TILES * D], BF16, name="own")
+            nc.sync.dma_start(out=own[:], in_=columns_of(own_rows, first, end))
             return neighbours, own
 
+        def part_of(filled, g):
+            width = filled.shape[1] // LOAD_GROUPS
+            return filled[:, (g % LOAD_GROUPS) * width : (g % LOAD_GROUPS + 1) * width]
+
         def mean_of_neighbours(neighbours):
-            both = neighbours[:].rearrange("p (r j d) -> p r j d", r=TILES, j=NEIGHBOURS)
+            both = neighbours.rearrange("p (r j d) -> p r j d", r=TILES, j=NEIGHBOURS)
             pair_sum = work.tile([P, TILES * D], BF16, name="pair_sum")
             nc.vector.tensor_tensor(
                 out=pair_sum[:].rearrange("p (r d) -> p r d", r=TILES),
@@ -88,7 +97,7 @@ def tile_graphsage_pa_t_kernel(tc, nf1, nf2, w1_0, w2_0, out):
             return mean
 
         def transpose_words(rows, r, name):
-            words = rows[:].bitcast(F32)
+            words = rows.bitcast(F32)
             bank = psum_t.tile([P, WORDS], F32, name=name)
             for g in range(PASSES):
                 for u in range(HALVES):
@@ -142,8 +151,8 @@ def tile_graphsage_pa_t_kernel(tc, nf1, nf2, w1_0, w2_0, out):
         identity = const.tile([P, P], F32, name="identity")
         make_identity(nc, identity[:])
         results = const.tile([P, GROUPS * TILES * H], F32, name="results")
-        loaded = [load(g) for g in range(LOAD_AHEAD)]
-        means = [mean_of_neighbours(loaded[0][0])]
+        loaded = [load(n) for n in range(LOADS_AHEAD)]
+        means = [mean_of_neighbours(part_of(loaded[0][0], 0))]
         w2_q = quantise_weight(nc, const, w2_0, nc.vector.tensor_copy, "w2")
         w1_q = quantise_weight(nc, const, w1_0, nc.scalar.copy, "w1")
 
@@ -151,17 +160,18 @@ def tile_graphsage_pa_t_kernel(tc, nf1, nf2, w1_0, w2_0, out):
         stored = 0
         for g in range(GROUPS + 1):
             if g + 1 < GROUPS:
-                means.append(mean_of_neighbours(loaded[g + 1][0]))
+                means.append(mean_of_neighbours(part_of(loaded[(g + 1) // LOAD_GROUPS][0], g + 1)))
             if g < GROUPS:
-                own_grouped = transpose_group(loaded[g][1], "own")
-                mean_grouped = transpose_group(means[g], "mean")
+                own_grouped = transpose_group(part_of(loaded[g // LOAD_GROUPS][1], g), "own")
+                mean_grouped = transpose_group(means[g][:], "mean")
                 own_q = quantise(own_grouped, "own")
                 mean_q = quantise(mean_grouped, "mean")
                 quantised.append((own_q, mean_q))
             if g > 0:
                 multiply(g - 1, quantised[g - 1][0], quantised[g - 1][1])
-            if g + LOAD_AHEAD < GROUPS:
-                loaded.append(load(g + LOAD_AHEAD))
+            if g // LOAD_GROUPS + LOADS_AHEAD < LOADS:
+                if (g + 1) % LOAD_GROUPS == 0:
+                    loaded.append(load(g // LOAD_GROUPS + LOADS_AHEAD))
             else:
                 nc.sync.dma_start(
                     out=columns_of(out_rows, stored, g), in_=columns_of(results, stored, g)

from contextlib import ExitStack

import concourse.mybir as mybir
from concourse.masks import make_identity

F32 = mybir.dt.float32
BF16 = mybir.dt.bfloat16
U32 = mybir.dt.uint32
U8 = mybir.dt.uint8
FP8X4 = mybir.dt.float8_e4m3fn_x4
ACT = mybir.ActivationFunctionType
ALU = mybir.AluOpType

P = 128
PACK = 4
K_PASS = P * PACK
HALVES = 2
PAIR = 2

NODES = 4096
NEIGHBOURS = 2
D = 1024
H = 256
PASSES = D // K_PASS
WORDS = D // PAIR

TILES = 2
GROUPS = NODES // (P * TILES)
LOAD_GROUPS = 2
LOADS = GROUPS // LOAD_GROUPS
LOADS_AHEAD = 3

FLOPS = 2 * 2 * NODES * D * H


def quantise_weight(nc, const, w, copy, name):
    raw = const.tile([P, PASSES * PACK * H], BF16, name=name + "_raw")
    nc.scalar.dma_start(
        out=raw[:].rearrange("p (s e c) -> p s e c", e=PAIR, c=H),
        in_=w.rearrange("(s p e) c -> p s e c", p=P, e=PAIR),
    )
    grouped = const.tile([P, PASSES * H * PACK], BF16, name=name + "_grouped", align_bytes=64)
    copy(
        out=grouped[:].rearrange("p (g c t) -> p g c t", g=PASSES, t=PACK),
        in_=raw[:].rearrange("p (g t c) -> p g c t", g=PASSES, t=PACK),
    )
    codes = const.tile([P, PASSES * H], U32, name=name + "_codes", align_bytes=64)
    scales = const.tile([P, PASSES * H], U8, name=name + "_scales", align_bytes=64)
    nc.vector.quantize_mx(out=codes[:].bitcast(FP8X4), scales=scales[:], in_=grouped[:])
    return codes, scales


def tile_graphsage_pa_t_kernel(tc, nf1, nf2, w1_0, w2_0, out):
    nc = tc.nc

    own_rows = nf1.rearrange("(p j) d -> p (j d)", p=P)
    neighbour_rows = nf2.rearrange("(p j) d -> p (j d)", p=P)
    out_rows = out.rearrange("(p j) h -> p (j h)", p=P)

    with ExitStack() as ctx:
        ctx.enter_context(tc.manual_schedule())
        const = ctx.enter_context(tc.tile_pool(name="const", bufs=1))
        loads = ctx.enter_context(tc.tile_pool(name="loads", bufs=LOADS_AHEAD))
        work = ctx.enter_context(tc.tile_pool(name="work", bufs=3))
        psum_t = ctx.enter_context(tc.psum_pool(name="psum_t", bufs=3))
        psum_acc = ctx.enter_context(tc.psum_pool(name="psum_acc", bufs=2))

        def columns_of(rows, first_group, end_group):
            width = rows.shape[1] // GROUPS
            return rows[:, first_group * width : end_group * width]

        def load(n):
            first, end = n * LOAD_GROUPS, (n + 1) * LOAD_GROUPS
            neighbours = loads.tile(
                [P, LOAD_GROUPS * TILES * NEIGHBOURS * D], BF16, name="neighbours"
            )
            nc.sync.dma_start(out=neighbours[:], in_=columns_of(neighbour_rows, first, end))
            own = loads.tile([P, LOAD_GROUPS * TILES * D], BF16, name="own")
            nc.sync.dma_start(out=own[:], in_=columns_of(own_rows, first, end))
            return neighbours, own

        def part_of(filled, g):
            width = filled.shape[1] // LOAD_GROUPS
            return filled[:, (g % LOAD_GROUPS) * width : (g % LOAD_GROUPS + 1) * width]

        def mean_of_neighbours(neighbours):
            both = neighbours.rearrange("p (r j d) -> p r j d", r=TILES, j=NEIGHBOURS)
            pair_sum = work.tile([P, TILES * D], BF16, name="pair_sum")
            nc.vector.tensor_tensor(
                out=pair_sum[:].rearrange("p (r d) -> p r d", r=TILES),
                in0=both[:, :, 0, :],
                in1=both[:, :, 1, :],
                op=ALU.add,
            )
            mean = work.tile([P, TILES * D], BF16, name="mean")
            nc.vector.tensor_scalar_mul(out=mean[:], in0=pair_sum[:], scalar1=1.0 / NEIGHBOURS)
            return mean

        def transpose_words(rows, r, name):
            words = rows.bitcast(F32)
            bank = psum_t.tile([P, WORDS], F32, name=name)
            for g in range(PASSES):
                for u in range(HALVES):
                    first = r * WORDS + (g * HALVES + u) * P
                    nc.tensor.transpose(
                        bank[:, (u * PASSES + g) * P : (u * PASSES + g + 1) * P],
                        words[:, first : first + P],
                        identity[:],
                    )
            return bank

        def transpose_group(rows, name):
            banks = [transpose_words(rows, r, name + "_t") for r in range(TILES)]
            grouped = work.tile([P, TILES * D], BF16, name=name + "_grouped", align_bytes=64)
            for r in range(TILES):
                nc.scalar.copy(
                    out=grouped[:]
                    .bitcast(F32)[:, r * WORDS : (r + 1) * WORDS]
                    .rearrange("p (n u) -> p n u", u=HALVES),
                    in_=banks[r][:].rearrange("p (u n) -> p n u", u=HALVES),
                )
            return grouped

        def quantise(grouped, name):
            codes = work.tile([P, TILES * D // PACK], U32, name=name + "_codes", align_bytes=64)
            scales = work.tile([P, TILES * D // PACK], U8, name=name + "_scales", align_bytes=64)
            nc.vector.quantize_mx(out=codes[:].bitcast(FP8X4), scales=scales[:], in_=grouped[:])
            return codes, scales

        def multiply(group, own_q, mean_q):
            products = ((own_q, w2_q), (mean_q, w1_q))
            acc = psum_acc.tile([P, TILES * H], F32, name="acc")
            for r in range(TILES):
                for i, (x_q, w_q) in enumerate(products):
                    for g in range(PASSES):
                        nodes = slice((r * PASSES + g) * P, (r * PASSES + g + 1) * P)
                        cols = slice(g * H, (g + 1) * H)
                        nc.tensor.matmul_mx(
                            out=acc[:, r * H : (r + 1) * H],
                            lhsT=x_q[0][:, nodes].bitcast(FP8X4),
                            lhsT_scale=x_q[1][:, nodes],
                            rhs=w_q[0][:, cols].bitcast(FP8X4),
                            rhs_scale=w_q[1][:, cols],
                            start=(i == 0 and g == 0),
                            stop=(i == len(products) - 1 and g == PASSES - 1),
                        )
            nc.scalar.activation(
                out=columns_of(results, group, group + 1), in_=acc[:], func=ACT.Relu
            )

        identity = const.tile([P, P], F32, name="identity")
        make_identity(nc, identity[:])
        results = const.tile([P, GROUPS * TILES * H], F32, name="results")
        loaded = [load(n) for n in range(LOADS_AHEAD)]
        means = [mean_of_neighbours(part_of(loaded[0][0], 0))]
        w2_q = quantise_weight(nc, const, w2_0, nc.vector.tensor_copy, "w2")
        w1_q = quantise_weight(nc, const, w1_0, nc.scalar.copy, "w1")

        quantised = []
        stored = 0
        for g in range(GROUPS + 1):
            if g + 1 < GROUPS:
                means.append(mean_of_neighbours(part_of(loaded[(g + 1) // LOAD_GROUPS][0], g + 1)))
            if g < GROUPS:
                own_grouped = transpose_group(part_of(loaded[g // LOAD_GROUPS][1], g), "own")
                mean_grouped = transpose_group(means[g][:], "mean")
                own_q = quantise(own_grouped, "own")
                mean_q = quantise(mean_grouped, "mean")
                quantised.append((own_q, mean_q))
            if g > 0:
                multiply(g - 1, quantised[g - 1][0], quantised[g - 1][1])
            if g // LOAD_GROUPS + LOADS_AHEAD < LOADS:
                if (g + 1) % LOAD_GROUPS == 0:
                    loaded.append(load(g // LOAD_GROUPS + LOADS_AHEAD))
            else:
                nc.sync.dma_start(
                    out=columns_of(out_rows, stored, g), in_=columns_of(results, stored, g)
                )
                stored = g
